import numpy as np
import ml_dtypes

BF16 = ml_dtypes.bfloat16


def bf(x):
    return np.asarray(x, np.float32).astype(BF16)


def f32(x):
    return np.asarray(x, np.float32)


def f64(x):
    return np.asarray(x).astype(np.float64)


def striped(idx):
    return np.tile(idx.reshape(-1, 16).T, (8, 1))


D, S, M, N = 128, 1024, 512, 512


def setup_inputs():
    return {"q": bf(np.random.standard_normal((D, M))), "keys": bf(np.random.standard_normal((D, N))), "wk": bf(np.random.standard_normal((D, D)) / np.sqrt(D)), "bk": f32(0.1 * np.random.standard_normal((D, 1))), "rel_k": bf(np.random.standard_normal((D, S))), "offs": striped(np.random.permutation(np.tile(np.arange(S), 2))[:N])}


def reference(q, keys, wk, bk, rel_k, offs):
    idx = offs[:16].T.reshape(-1)
    kk = f64(wk).T @ f64(keys) + f64(bk)
    return (f64(q).T @ kk + f64(q).T @ f64(rel_k)[:, idx]) / np.sqrt(D)

@@ -1,0 +1,58 @@
+import math
+
+import concourse.mybir as mybir
+
+BF16, F32, U16 = mybir.dt.bfloat16, mybir.dt.float32, mybir.dt.uint16
+
+P = 128
+D, S, M, N = 128, 1024, 512, 512
+M_BLOCKS = M // P
+
+FLOPS = 2 * D * D * N + 2 * (2 * D * M * N)
+
+
+def tile_pointerwithrelations_kernel(tc, q, keys, wk, bk, rel_k, offs, out):
+    nc = tc.nc
+    with (
+        tc.tile_pool(name="held", bufs=1) as held,
+        tc.tile_pool(name="staging", bufs=M_BLOCKS) as staging,
+        tc.psum_pool(name="psum", bufs=1) as psum,
+    ):
+        offsets = held.tile([P, N // 16], U16, name="offsets")
+        nc.sync.dma_start(offsets[:], offs)
+        table = held.tile([P, S], BF16, name="table")
+        nc.sync.dma_start(table[:], rel_k)
+        queries = held.tile([P, M], BF16, name="queries")
+        nc.sync.dma_start(queries[:], q)
+        weights = held.tile([P, D], BF16, name="weights")
+        nc.scalar.dma_start(weights[:], wk)
+        raw_keys = held.tile([P, N], BF16, name="raw_keys")
+        nc.scalar.dma_start(raw_keys[:], keys)
+        bias = held.tile([P, 1], F32, name="bias")
+        nc.scalar.dma_start(bias[:], bk)
+
+        kk_bank = psum.tile([P, N], F32, name="kk_bank")
+        nc.tensor.matmul(kk_bank[:], weights[:], raw_keys[:], start=True, stop=True)
+        kk = held.tile([P, N], BF16, name="kk")
+        nc.vector.tensor_scalar_add(kk[:], kk_bank[:], bias[:, 0:1])
+
+        banks = [psum.tile([P, N], F32, name=f"bank{b}") for b in range(M_BLOCKS)]
+        for b in range(M_BLOCKS):
+            nc.tensor.matmul(
+                banks[b][:],
+                queries[:, b * P : (b + 1) * P],
+                table[:].indirect(offsets[:]),
+                start=True,
+                stop=False,
+            )
+
+        for b in range(M_BLOCKS):
+            nc.tensor.matmul(
+                banks[b][:], queries[:, b * P : (b + 1) * P], kk[:], start=False, stop=True
+            )
+            scores = staging.tile([P, N], F32, name="scores")
+            if b % 2 == 0:
+                nc.vector.tensor_scalar_mul(scores[:], banks[b][:], 1.0 / math.sqrt(D))
+            else:
+                nc.scalar.mul(scores[:], banks[b][:], 1.0 / math.sqrt(D))
+            nc.sync.dma_start(out[b * P : (b + 1) * P, :], scores[:])

@@ -7,6 +7,7 @@ BF16, F32, U16 = mybir.dt.bfloat16, mybir.dt.float32, mybir.dt.uint16
 P = 128
 D, S, M, N = 128, 1024, 512, 512
 M_BLOCKS = M // P
+WARMUP = 6
 
 FLOPS = 2 * D * D * N + 2 * (2 * D * M * N)
 
@@ -30,6 +31,12 @@ def tile_pointerwithrelations_kernel(tc, q, keys, wk, bk, rel_k, offs, out):
         nc.scalar.dma_start(raw_keys[:], keys)
         bias = held.tile([P, 1], F32, name="bias")
         nc.scalar.dma_start(bias[:], bk)
+
+        zeros = held.tile([P, N], BF16, name="zeros")
+        nc.vector.memset(zeros[:], 0.0)
+        warm_bank = psum.tile([P, N], F32, name="warm_bank")
+        for w in range(WARMUP):
+            nc.tensor.matmul(warm_bank[:], zeros[:, 0:P], zeros[:], start=True, stop=True)
 
         kk_bank = psum.tile([P, N], F32, name="kk_bank")
         nc.tensor.matmul(kk_bank[:], weights[:], raw_keys[:], start=True, stop=True)

@@ -7,7 +7,6 @@ BF16, F32, U16 = mybir.dt.bfloat16, mybir.dt.float32, mybir.dt.uint16
 P = 128
 D, S, M, N = 128, 1024, 512, 512
 M_BLOCKS = M // P
-WARMUP = 6
 
 FLOPS = 2 * D * D * N + 2 * (2 * D * M * N)
 
@@ -23,20 +22,14 @@ def tile_pointerwithrelations_kernel(tc, q, keys, wk, bk, rel_k, offs, out):
         nc.sync.dma_start(offsets[:], offs)
         table = held.tile([P, S], BF16, name="table")
         nc.sync.dma_start(table[:], rel_k)
-        queries = held.tile([P, M], BF16, name="queries")
-        nc.sync.dma_start(queries[:], q)
         weights = held.tile([P, D], BF16, name="weights")
         nc.scalar.dma_start(weights[:], wk)
         raw_keys = held.tile([P, N], BF16, name="raw_keys")
         nc.scalar.dma_start(raw_keys[:], keys)
+        queries = held.tile([P, M], BF16, name="queries")
+        nc.gpsimd.dma_start(queries[:], q)
         bias = held.tile([P, 1], F32, name="bias")
-        nc.scalar.dma_start(bias[:], bk)
-
-        zeros = held.tile([P, N], BF16, name="zeros")
-        nc.vector.memset(zeros[:], 0.0)
-        warm_bank = psum.tile([P, N], F32, name="warm_bank")
-        for w in range(WARMUP):
-            nc.tensor.matmul(warm_bank[:], zeros[:, 0:P], zeros[:], start=True, stop=True)
+        nc.gpsimd.dma_start(bias[:], bk)
 
         kk_bank = psum.tile([P, N], F32, name="kk_bank")
         nc.tensor.matmul(kk_bank[:], weights[:], raw_keys[:], start=True, stop=True)

@@ -7,6 +7,7 @@ BF16, F32, U16 = mybir.dt.bfloat16, mybir.dt.float32, mybir.dt.uint16
 P = 128
 D, S, M, N = 128, 1024, 512, 512
 M_BLOCKS = M // P
+WARMUP = 16
 
 FLOPS = 2 * D * D * N + 2 * (2 * D * M * N)
 
@@ -22,14 +23,20 @@ def tile_pointerwithrelations_kernel(tc, q, keys, wk, bk, rel_k, offs, out):
         nc.sync.dma_start(offsets[:], offs)
         table = held.tile([P, S], BF16, name="table")
         nc.sync.dma_start(table[:], rel_k)
+        queries = held.tile([P, M], BF16, name="queries")
+        nc.sync.dma_start(queries[:], q)
         weights = held.tile([P, D], BF16, name="weights")
         nc.scalar.dma_start(weights[:], wk)
         raw_keys = held.tile([P, N], BF16, name="raw_keys")
         nc.scalar.dma_start(raw_keys[:], keys)
-        queries = held.tile([P, M], BF16, name="queries")
-        nc.gpsimd.dma_start(queries[:], q)
         bias = held.tile([P, 1], F32, name="bias")
-        nc.gpsimd.dma_start(bias[:], bk)
+        nc.scalar.dma_start(bias[:], bk)
+
+        zeros = held.tile([P, P], BF16, name="zeros")
+        nc.vector.memset(zeros[:], 0.0)
+        warm_bank = psum.tile([P, P], F32, name="warm_bank")
+        for w in range(WARMUP):
+            nc.tensor.matmul(warm_bank[:], zeros[:], zeros[:], start=True, stop=True)
 
         kk_bank = psum.tile([P, N], F32, name="kk_bank")
         nc.tensor.matmul(kk_bank[:], weights[:], raw_keys[:], start=True, stop=True)

@@ -7,7 +7,6 @@ BF16, F32, U16 = mybir.dt.bfloat16, mybir.dt.float32, mybir.dt.uint16
 P = 128
 D, S, M, N = 128, 1024, 512, 512
 M_BLOCKS = M // P
-WARMUP = 16
 
 FLOPS = 2 * D * D * N + 2 * (2 * D * M * N)
 
@@ -19,24 +18,18 @@ def tile_pointerwithrelations_kernel(tc, q, keys, wk, bk, rel_k, offs, out):
         tc.tile_pool(name="staging", bufs=M_BLOCKS) as staging,
         tc.psum_pool(name="psum", bufs=1) as psum,
     ):
-        offsets = held.tile([P, N // 16], U16, name="offsets")
-        nc.sync.dma_start(offsets[:], offs)
-        table = held.tile([P, S], BF16, name="table")
-        nc.sync.dma_start(table[:], rel_k)
-        queries = held.tile([P, M], BF16, name="queries")
-        nc.sync.dma_start(queries[:], q)
+        raw_keys = held.tile([P, N], BF16, name="raw_keys")
+        nc.sync.dma_start(raw_keys[:], keys)
         weights = held.tile([P, D], BF16, name="weights")
         nc.scalar.dma_start(weights[:], wk)
-        raw_keys = held.tile([P, N], BF16, name="raw_keys")
-        nc.scalar.dma_start(raw_keys[:], keys)
+        offsets = held.tile([P, N // 16], U16, name="offsets")
+        nc.sync.dma_start(offsets[:], offs)
+        queries = held.tile([P, M], BF16, name="queries")
+        nc.scalar.dma_start(queries[:], q)
+        table = held.tile([P, S], BF16, name="table")
+        nc.sync.dma_start(table[:], rel_k)
         bias = held.tile([P, 1], F32, name="bias")
         nc.scalar.dma_start(bias[:], bk)
-
-        zeros = held.tile([P, P], BF16, name="zeros")
-        nc.vector.memset(zeros[:], 0.0)
-        warm_bank = psum.tile([P, P], F32, name="warm_bank")
-        for w in range(WARMUP):
-            nc.tensor.matmul(warm_bank[:], zeros[:], zeros[:], start=True, stop=True)
 
         kk_bank = psum.tile([P, N], F32, name="kk_bank")
         nc.tensor.matmul(kk_bank[:], weights[:], raw_keys[:], start=True, stop=True)

@@ -7,6 +7,7 @@ BF16, F32, U16 = mybir.dt.bfloat16, mybir.dt.float32, mybir.dt.uint16
 P = 128
 D, S, M, N = 128, 1024, 512, 512
 M_BLOCKS = M // P
+CLOSING_PIECES = 8
 
 FLOPS = 2 * D * D * N + 2 * (2 * D * M * N)
 
@@ -17,6 +18,7 @@ def tile_pointerwithrelations_kernel(tc, q, keys, wk, bk, rel_k, offs, out):
         tc.tile_pool(name="held", bufs=1) as held,
         tc.tile_pool(name="staging", bufs=M_BLOCKS) as staging,
         tc.psum_pool(name="psum", bufs=1) as psum,
+        tc.psum_pool(name="ring", bufs=M_BLOCKS - 1) as ring,
     ):
         raw_keys = held.tile([P, N], BF16, name="raw_keys")
         nc.sync.dma_start(raw_keys[:], keys)
@@ -36,8 +38,9 @@ def tile_pointerwithrelations_kernel(tc, q, keys, wk, bk, rel_k, offs, out):
         kk = held.tile([P, N], BF16, name="kk")
         nc.vector.tensor_scalar_add(kk[:], kk_bank[:], bias[:, 0:1])
 
-        banks = [psum.tile([P, N], F32, name=f"bank{b}") for b in range(M_BLOCKS)]
+        banks = {}
         for b in range(M_BLOCKS):
+            banks[b] = ring.tile([P, N], F32, name="bank")
             nc.tensor.matmul(
                 banks[b][:],
                 queries[:, b * P : (b + 1) * P],
@@ -47,9 +50,17 @@ def tile_pointerwithrelations_kernel(tc, q, keys, wk, bk, rel_k, offs, out):
             )
 
         for b in range(M_BLOCKS):
-            nc.tensor.matmul(
-                banks[b][:], queries[:, b * P : (b + 1) * P], kk[:], start=False, stop=True
-            )
+            pieces = CLOSING_PIECES if b < M_BLOCKS - 1 else 1
+            width = N // pieces
+            for piece in range(pieces):
+                columns = slice(piece * width, (piece + 1) * width)
+                nc.tensor.matmul(
+                    banks[b][:, columns],
+                    queries[:, b * P : (b + 1) * P],
+                    kk[:, columns],
+                    start=False,
+                    stop=(piece == pieces - 1),
+                )
             scores = staging.tile([P, N], F32, name="scores")
             if b % 2 == 0:
                 nc.vector.tensor_scalar_mul(scores[:], banks[b][:], 1.0 / math.sqrt(D))

@@ -64,6 +64,12 @@ def tile_pointerwithrelations_kernel(tc, q, keys, wk, bk, rel_k, offs, out):
             scores = staging.tile([P, N], F32, name="scores")
             if b % 2 == 0:
                 nc.vector.tensor_scalar_mul(scores[:], banks[b][:], 1.0 / math.sqrt(D))
-            else:
+                nc.sync.dma_start(out[b * P : (b + 1) * P, :], scores[:])
+            elif b < M_BLOCKS - 1:
                 nc.scalar.mul(scores[:], banks[b][:], 1.0 / math.sqrt(D))
-            nc.sync.dma_start(out[b * P : (b + 1) * P, :], scores[:])
+                nc.sync.dma_start(out[b * P : (b + 1) * P, :], scores[:])
+            else:
+                for half in range(2):
+                    columns = slice(half * (N // 2), (half + 1) * (N // 2))
+                    nc.scalar.mul(scores[:, columns], banks[b][:, columns], 1.0 / math.sqrt(D))
+                    nc.sync.dma_start(out[b * P : (b + 1) * P, columns], scores[:, columns])

@@ -18,7 +18,6 @@ def tile_pointerwithrelations_kernel(tc, q, keys, wk, bk, rel_k, offs, out):
         tc.tile_pool(name="held", bufs=1) as held,
         tc.tile_pool(name="staging", bufs=M_BLOCKS) as staging,
         tc.psum_pool(name="psum", bufs=1) as psum,
-        tc.psum_pool(name="ring", bufs=M_BLOCKS - 1) as ring,
     ):
         raw_keys = held.tile([P, N], BF16, name="raw_keys")
         nc.sync.dma_start(raw_keys[:], keys)
@@ -38,9 +37,9 @@ def tile_pointerwithrelations_kernel(tc, q, keys, wk, bk, rel_k, offs, out):
         kk = held.tile([P, N], BF16, name="kk")
         nc.vector.tensor_scalar_add(kk[:], kk_bank[:], bias[:, 0:1])
 
-        banks = {}
-        for b in range(M_BLOCKS):
-            banks[b] = ring.tile([P, N], F32, name="bank")
+        early = range(M_BLOCKS - 1)
+        banks = [psum.tile([P, N], F32, name=f"bank{b}") for b in early]
+        for b in early:
             nc.tensor.matmul(
                 banks[b][:],
                 queries[:, b * P : (b + 1) * P],
@@ -49,27 +48,51 @@ def tile_pointerwithrelations_kernel(tc, q, keys, wk, bk, rel_k, offs, out):
                 stop=False,
             )
 
-        for b in range(M_BLOCKS):
-            pieces = CLOSING_PIECES if b < M_BLOCKS - 1 else 1
-            width = N // pieces
-            for piece in range(pieces):
+        width = N // CLOSING_PIECES
+        for b in early:
+            for piece in range(CLOSING_PIECES):
                 columns = slice(piece * width, (piece + 1) * width)
                 nc.tensor.matmul(
                     banks[b][:, columns],
                     queries[:, b * P : (b + 1) * P],
                     kk[:, columns],
                     start=False,
-                    stop=(piece == pieces - 1),
+                    stop=(piece == CLOSING_PIECES - 1),
                 )
             scores = staging.tile([P, N], F32, name="scores")
+            if b == 0:
+                for h in range(2):
+                    columns = slice(h * (N // 2), (h + 1) * (N // 2))
+                    nc.vector.tensor_scalar_mul(
+                        scores[:, columns], banks[b][:, columns], 1.0 / math.sqrt(D)
+                    )
+                    nc.sync.dma_start(out[b * P : (b + 1) * P, columns], scores[:, columns])
+                continue
             if b % 2 == 0:
                 nc.vector.tensor_scalar_mul(scores[:], banks[b][:], 1.0 / math.sqrt(D))
-                nc.sync.dma_start(out[b * P : (b + 1) * P, :], scores[:])
-            elif b < M_BLOCKS - 1:
-                nc.scalar.mul(scores[:], banks[b][:], 1.0 / math.sqrt(D))
-                nc.sync.dma_start(out[b * P : (b + 1) * P, :], scores[:])
             else:
-                for half in range(2):
-                    columns = slice(half * (N // 2), (half + 1) * (N // 2))
-                    nc.scalar.mul(scores[:, columns], banks[b][:, columns], 1.0 / math.sqrt(D))
-                    nc.sync.dma_start(out[b * P : (b + 1) * P, columns], scores[:, columns])
+                nc.scalar.mul(scores[:], banks[b][:], 1.0 / math.sqrt(D))
+            nc.sync.dma_start(out[b * P : (b + 1) * P, :], scores[:])
+
+        last = M_BLOCKS - 1
+        half_banks = [psum.tile([P, N // 2], F32, name=f"half_bank{h}") for h in range(2)]
+        for h in range(2):
+            nc.tensor.matmul(
+                half_banks[h][:],
+                queries[:, last * P : M],
+                kk[:, h * (N // 2) : (h + 1) * (N // 2)],
+                start=True,
+                stop=False,
+            )
+        for h in range(2):
+            columns = slice(h * (N // 2), (h + 1) * (N // 2))
+            nc.tensor.matmul(
+                half_banks[h][:],
+                queries[:, last * P : M],
+                table[:].indirect(offsets[:, h * (N // 32) : (h + 1) * (N // 32)]),
+                start=False,
+                stop=True,
+            )
+            half_scores = staging.tile([P, N // 2], F32, name="half_scores")
+            nc.scalar.mul(half_scores[:], half_banks[h][:], 1.0 / math.sqrt(D))
+            nc.sync.dma_start(out[last * P : M, columns], half_scores[:])

@@ -75,24 +75,23 @@ def tile_pointerwithrelations_kernel(tc, q, keys, wk, bk, rel_k, offs, out):
             nc.sync.dma_start(out[b * P : (b + 1) * P, :], scores[:])
 
         last = M_BLOCKS - 1
-        half_banks = [psum.tile([P, N // 2], F32, name=f"half_bank{h}") for h in range(2)]
-        for h in range(2):
+        cuts = (0, 3 * N // 4, N)
+        parts = [slice(cuts[i], cuts[i + 1]) for i in range(2)]
+        part_banks = [
+            psum.tile([P, cuts[i + 1] - cuts[i]], F32, name=f"part_bank{i}") for i in range(2)
+        ]
+        for i in range(2):
             nc.tensor.matmul(
-                half_banks[h][:],
-                queries[:, last * P : M],
-                kk[:, h * (N // 2) : (h + 1) * (N // 2)],
-                start=True,
-                stop=False,
+                part_banks[i][:], queries[:, last * P : M], kk[:, parts[i]], start=True, stop=False
             )
-        for h in range(2):
-            columns = slice(h * (N // 2), (h + 1) * (N // 2))
+        for i in range(2):
             nc.tensor.matmul(
-                half_banks[h][:],
+                part_banks[i][:],
                 queries[:, last * P : M],
-                table[:].indirect(offsets[:, h * (N // 32) : (h + 1) * (N // 32)]),
+                table[:].indirect(offsets[:, cuts[i] // 16 : cuts[i + 1] // 16]),
                 start=False,
                 stop=True,
             )
-            half_scores = staging.tile([P, N // 2], F32, name="half_scores")
-            nc.scalar.mul(half_scores[:], half_banks[h][:], 1.0 / math.sqrt(D))
-            nc.sync.dma_start(out[last * P : M, columns], half_scores[:])
+            part_scores = held.tile([P, cuts[i + 1] - cuts[i]], F32, name=f"part_scores{i}")
+            nc.scalar.mul(part_scores[:], part_banks[i][:], 1.0 / math.sqrt(D))
+            nc.sync.dma_start(out[last * P : M, parts[i]], part_scores[:])

@@ -7,7 +7,8 @@ BF16, F32, U16 = mybir.dt.bfloat16, mybir.dt.float32, mybir.dt.uint16
 P = 128
 D, S, M, N = 128, 1024, 512, 512
 M_BLOCKS = M // P
-CLOSING_PIECES = 8
+EARLY = 2
+PIECE = 48
 
 FLOPS = 2 * D * D * N + 2 * (2 * D * M * N)
 
@@ -16,7 +17,7 @@ def tile_pointerwithrelations_kernel(tc, q, keys, wk, bk, rel_k, offs, out):
     nc = tc.nc
     with (
         tc.tile_pool(name="held", bufs=1) as held,
-        tc.tile_pool(name="staging", bufs=M_BLOCKS) as staging,
+        tc.tile_pool(name="staging", bufs=EARLY) as staging,
         tc.psum_pool(name="psum", bufs=1) as psum,
     ):
         raw_keys = held.tile([P, N], BF16, name="raw_keys")
@@ -37,9 +38,8 @@ def tile_pointerwithrelations_kernel(tc, q, keys, wk, bk, rel_k, offs, out):
         kk = held.tile([P, N], BF16, name="kk")
         nc.vector.tensor_scalar_add(kk[:], kk_bank[:], bias[:, 0:1])
 
-        early = range(M_BLOCKS - 1)
-        banks = [psum.tile([P, N], F32, name=f"bank{b}") for b in early]
-        for b in early:
+        banks = [psum.tile([P, N], F32, name=f"bank{b}") for b in range(EARLY)]
+        for b in range(EARLY):
             nc.tensor.matmul(
                 banks[b][:],
                 queries[:, b * P : (b + 1) * P],
@@ -48,50 +48,48 @@ def tile_pointerwithrelations_kernel(tc, q, keys, wk, bk, rel_k, offs, out):
                 stop=False,
             )
 
-        width = N // CLOSING_PIECES
-        for b in early:
-            for piece in range(CLOSING_PIECES):
-                columns = slice(piece * width, (piece + 1) * width)
+        for b in range(EARLY):
+            for first in range(0, N, PIECE):
+                columns = slice(first, min(first + PIECE, N))
                 nc.tensor.matmul(
                     banks[b][:, columns],
                     queries[:, b * P : (b + 1) * P],
                     kk[:, columns],
                     start=False,
-                    stop=(piece == CLOSING_PIECES - 1),
+                    stop=(first + PIECE >= N),
                 )
             scores = staging.tile([P, N], F32, name="scores")
-            if b == 0:
-                for h in range(2):
-                    columns = slice(h * (N // 2), (h + 1) * (N // 2))
-                    nc.vector.tensor_scalar_mul(
-                        scores[:, columns], banks[b][:, columns], 1.0 / math.sqrt(D)
-                    )
-                    nc.sync.dma_start(out[b * P : (b + 1) * P, columns], scores[:, columns])
-                continue
             if b % 2 == 0:
                 nc.vector.tensor_scalar_mul(scores[:], banks[b][:], 1.0 / math.sqrt(D))
             else:
                 nc.scalar.mul(scores[:], banks[b][:], 1.0 / math.sqrt(D))
             nc.sync.dma_start(out[b * P : (b + 1) * P, :], scores[:])
 
-        last = M_BLOCKS - 1
         cuts = (0, 3 * N // 4, N)
-        parts = [slice(cuts[i], cuts[i + 1]) for i in range(2)]
-        part_banks = [
-            psum.tile([P, cuts[i + 1] - cuts[i]], F32, name=f"part_bank{i}") for i in range(2)
-        ]
-        for i in range(2):
+        late = [(b, i) for b in range(EARLY, M_BLOCKS) for i in range(2)]
+        part_banks = {
+            (b, i): psum.tile([P, cuts[i + 1] - cuts[i]], F32, name=f"part_bank{b}_{i}")
+            for b, i in late
+        }
+        for b, i in late:
             nc.tensor.matmul(
-                part_banks[i][:], queries[:, last * P : M], kk[:, parts[i]], start=True, stop=False
+                part_banks[b, i][:],
+                queries[:, b * P : (b + 1) * P],
+                kk[:, cuts[i] : cuts[i + 1]],
+                start=True,
+                stop=False,
             )
-        for i in range(2):
+        for b, i in late:
             nc.tensor.matmul(
-                part_banks[i][:],
-                queries[:, last * P : M],
+                part_banks[b, i][:],
+                queries[:, b * P : (b + 1) * P],
                 table[:].indirect(offsets[:, cuts[i] // 16 : cuts[i + 1] // 16]),
                 start=False,
                 stop=True,
             )
-            part_scores = held.tile([P, cuts[i + 1] - cuts[i]], F32, name=f"part_scores{i}")
-            nc.scalar.mul(part_scores[:], part_banks[i][:], 1.0 / math.sqrt(D))
-            nc.sync.dma_start(out[last * P : M, parts[i]], part_scores[:])
+            part_scores = held.tile([P, cuts[i + 1] - cuts[i]], F32, name=f"part_scores{b}_{i}")
+            if b % 2 == 0:
+                nc.vector.tensor_scalar_mul(part_scores[:], part_banks[b, i][:], 1.0 / math.sqrt(D))
+            else:
+                nc.scalar.mul(part_scores[:], part_banks[b, i][:], 1.0 / math.sqrt(D))
+            nc.sync.dma_start(out[b * P : (b + 1) * P, cuts[i] : cuts[i + 1]], part_scores[:])

@@ -26,26 +26,36 @@ def tile_pointerwithrelations_kernel(tc, q, keys, wk, bk, rel_k, offs, out):
         nc.scalar.dma_start(weights[:], wk)
         offsets = held.tile([P, N // 16], U16, name="offsets")
         nc.sync.dma_start(offsets[:], offs)
-        queries = held.tile([P, M], BF16, name="queries")
-        nc.scalar.dma_start(queries[:], q)
+        first_queries = held.tile([P, P], BF16, name="first_queries")
+        nc.scalar.dma_start(first_queries[:], q[:, 0:P])
         table = held.tile([P, S], BF16, name="table")
         nc.sync.dma_start(table[:], rel_k)
+        other_queries = held.tile([P, M - P], BF16, name="other_queries")
+        nc.sync.dma_start(other_queries[:], q[:, P:M])
         bias = held.tile([P, 1], F32, name="bias")
         nc.scalar.dma_start(bias[:], bk)
+        queries = [first_queries[:]] + [
+            other_queries[:, b * P : (b + 1) * P] for b in range(M_BLOCKS - 1)
+        ]
 
         kk_bank = psum.tile([P, N], F32, name="kk_bank")
         nc.tensor.matmul(kk_bank[:], weights[:], raw_keys[:], start=True, stop=True)
         kk = held.tile([P, N], BF16, name="kk")
         nc.vector.tensor_scalar_add(kk[:], kk_bank[:], bias[:, 0:1])
 
+        def store_scaled(b, columns, bank, scores):
+            rows = out[b * P : (b + 1) * P, columns]
+            if b % 2 == 0:
+                nc.vector.tensor_scalar_mul(scores, bank, 1.0 / math.sqrt(D))
+                nc.sync.dma_start(rows, scores)
+            else:
+                nc.scalar.mul(scores, bank, 1.0 / math.sqrt(D))
+                nc.scalar.dma_start(rows, scores)
+
         banks = [psum.tile([P, N], F32, name=f"bank{b}") for b in range(EARLY)]
         for b in range(EARLY):
             nc.tensor.matmul(
-                banks[b][:],
-                queries[:, b * P : (b + 1) * P],
-                table[:].indirect(offsets[:]),
-                start=True,
-                stop=False,
+                banks[b][:], queries[b], table[:].indirect(offsets[:]), start=True, stop=False
             )
 
         for b in range(EARLY):
@@ -53,17 +63,15 @@ def tile_pointerwithrelations_kernel(tc, q, keys, wk, bk, rel_k, offs, out):
                 columns = slice(first, min(first + PIECE, N))
                 nc.tensor.matmul(
                     banks[b][:, columns],
-                    queries[:, b * P : (b + 1) * P],
+                    queries[b],
                     kk[:, columns],
                     start=False,
                     stop=(first + PIECE >= N),
                 )
             scores = staging.tile([P, N], F32, name="scores")
-            if b % 2 == 0:
-                nc.vector.tensor_scalar_mul(scores[:], banks[b][:], 1.0 / math.sqrt(D))
-            else:
-                nc.scalar.mul(scores[:], banks[b][:], 1.0 / math.sqrt(D))
-            nc.sync.dma_start(out[b * P : (b + 1) * P, :], scores[:])
+            for h in range(2):
+                columns = slice(h * (N // 2), (h + 1) * (N // 2))
+                store_scaled(b, columns, banks[b][:, columns], scores[:, columns])
 
         cuts = (0, 3 * N // 4, N)
         late = [(b, i) for b in range(EARLY, M_BLOCKS) for i in range(2)]
@@ -74,7 +82,7 @@ def tile_pointerwithrelations_kernel(tc, q, keys, wk, bk, rel_k, offs, out):
         for b, i in late:
             nc.tensor.matmul(
                 part_banks[b, i][:],
-                queries[:, b * P : (b + 1) * P],
+                queries[b],
                 kk[:, cuts[i] : cuts[i + 1]],
                 start=True,
                 stop=False,
@@ -82,14 +90,10 @@ def tile_pointerwithrelations_kernel(tc, q, keys, wk, bk, rel_k, offs, out):
         for b, i in late:
             nc.tensor.matmul(
                 part_banks[b, i][:],
-                queries[:, b * P : (b + 1) * P],
+                queries[b],
                 table[:].indirect(offsets[:, cuts[i] // 16 : cuts[i + 1] // 16]),
                 start=False,
                 stop=True,
             )
             part_scores = held.tile([P, cuts[i + 1] - cuts[i]], F32, name=f"part_scores{b}_{i}")
-            if b % 2 == 0:
-                nc.vector.tensor_scalar_mul(part_scores[:], part_banks[b, i][:], 1.0 / math.sqrt(D))
-            else:
-                nc.scalar.mul(part_scores[:], part_banks[b, i][:], 1.0 / math.sqrt(D))
-            nc.sync.dma_start(out[b * P : (b + 1) * P, cuts[i] : cuts[i + 1]], part_scores[:])
+            store_scaled(b, slice(cuts[i], cuts[i + 1]), part_banks[b, i][:], part_scores[:])

@@ -20,10 +20,12 @@ def tile_pointerwithrelations_kernel(tc, q, keys, wk, bk, rel_k, offs, out):
         tc.tile_pool(name="staging", bufs=EARLY) as staging,
         tc.psum_pool(name="psum", bufs=1) as psum,
     ):
-        raw_keys = held.tile([P, N], BF16, name="raw_keys")
-        nc.sync.dma_start(raw_keys[:], keys)
         weights = held.tile([P, D], BF16, name="weights")
-        nc.scalar.dma_start(weights[:], wk)
+        nc.sync.dma_start(weights[:], wk)
+        halves = (slice(0, N // 2), slice(N // 2, N))
+        raw_keys = [held.tile([P, N // 2], BF16, name=f"raw_keys{h}") for h in range(2)]
+        nc.scalar.dma_start(raw_keys[0][:], keys[:, halves[0]])
+        nc.sync.dma_start(raw_keys[1][:], keys[:, halves[1]])
         offsets = held.tile([P, N // 16], U16, name="offsets")
         nc.sync.dma_start(offsets[:], offs)
         first_queries = held.tile([P, P], BF16, name="first_queries")
@@ -33,13 +35,14 @@ def tile_pointerwithrelations_kernel(tc, q, keys, wk, bk, rel_k, offs, out):
         other_queries = held.tile([P, M - P], BF16, name="other_queries")
         nc.sync.dma_start(other_queries[:], q[:, P:M])
         bias = held.tile([P, 1], F32, name="bias")
-        nc.scalar.dma_start(bias[:], bk)
+        nc.sync.dma_start(bias[:], bk)
         queries = [first_queries[:]] + [
             other_queries[:, b * P : (b + 1) * P] for b in range(M_BLOCKS - 1)
         ]
 
         kk_bank = psum.tile([P, N], F32, name="kk_bank")
-        nc.tensor.matmul(kk_bank[:], weights[:], raw_keys[:], start=True, stop=True)
+        for half, half_keys in zip(halves, raw_keys):
+            nc.tensor.matmul(kk_bank[:, half], weights[:], half_keys[:], start=True, stop=True)
         kk = held.tile([P, N], BF16, name="kk")
         nc.vector.tensor_scalar_add(kk[:], kk_bank[:], bias[:, 0:1])
 
@@ -69,31 +72,29 @@ def tile_pointerwithrelations_kernel(tc, q, keys, wk, bk, rel_k, offs, out):
                     stop=(first + PIECE >= N),
                 )
             scores = staging.tile([P, N], F32, name="scores")
-            for h in range(2):
-                columns = slice(h * (N // 2), (h + 1) * (N // 2))
+            for columns in halves:
                 store_scaled(b, columns, banks[b][:, columns], scores[:, columns])
 
-        cuts = (0, 3 * N // 4, N)
-        late = [(b, i) for b in range(EARLY, M_BLOCKS) for i in range(2)]
-        part_banks = {
-            (b, i): psum.tile([P, cuts[i + 1] - cuts[i]], F32, name=f"part_bank{b}_{i}")
+        late = [(b, i) for i in range(2) for b in range(EARLY, M_BLOCKS)]
+        half_banks = {
+            (b, i): psum.tile([P, N // 2], F32, name=f"half_bank{b}_{i}")
             for b, i in late
         }
         for b, i in late:
             nc.tensor.matmul(
-                part_banks[b, i][:],
+                half_banks[b, i][:],
                 queries[b],
-                kk[:, cuts[i] : cuts[i + 1]],
+                kk[:, halves[i]],
                 start=True,
                 stop=False,
             )
         for b, i in late:
             nc.tensor.matmul(
-                part_banks[b, i][:],
+                half_banks[b, i][:],
                 queries[b],
-                table[:].indirect(offsets[:, cuts[i] // 16 : cuts[i + 1] // 16]),
+                table[:].indirect(offsets[:, halves[i].start // 16 : halves[i].stop // 16]),
                 start=False,
                 stop=True,
             )
-            part_scores = held.tile([P, cuts[i + 1] - cuts[i]], F32, name=f"part_scores{b}_{i}")
-            store_scaled(b, slice(cuts[i], cuts[i + 1]), part_banks[b, i][:], part_scores[:])
+            half_scores = held.tile([P, N // 2], F32, name=f"half_scores{b}_{i}")
+            store_scaled(b, halves[i], half_banks[b, i][:], half_scores[:])

import math

import concourse.mybir as mybir

BF16, F32, U16 = mybir.dt.bfloat16, mybir.dt.float32, mybir.dt.uint16

P = 128
D, S, M, N = 128, 1024, 512, 512
M_BLOCKS = M // P
EARLY = 2
PIECE = 48

FLOPS = 2 * D * D * N + 2 * (2 * D * M * N)


def tile_pointerwithrelations_kernel(tc, q, keys, wk, bk, rel_k, offs, out):
    nc = tc.nc
    with (
        tc.tile_pool(name="held", bufs=1) as held,
        tc.tile_pool(name="staging", bufs=EARLY) as staging,
        tc.psum_pool(name="psum", bufs=1) as psum,
    ):
        weights = held.tile([P, D], BF16, name="weights")
        nc.sync.dma_start(weights[:], wk)
        halves = (slice(0, N // 2), slice(N // 2, N))
        raw_keys = [held.tile([P, N // 2], BF16, name=f"raw_keys{h}") for h in range(2)]
        nc.scalar.dma_start(raw_keys[0][:], keys[:, halves[0]])
        nc.sync.dma_start(raw_keys[1][:], keys[:, halves[1]])
        offsets = held.tile([P, N // 16], U16, name="offsets")
        nc.sync.dma_start(offsets[:], offs)
        first_queries = held.tile([P, P], BF16, name="first_queries")
        nc.scalar.dma_start(first_queries[:], q[:, 0:P])
        table = held.tile([P, S], BF16, name="table")
        nc.sync.dma_start(table[:], rel_k)
        other_queries = held.tile([P, M - P], BF16, name="other_queries")
        nc.sync.dma_start(other_queries[:], q[:, P:M])
        bias = held.tile([P, 1], F32, name="bias")
        nc.sync.dma_start(bias[:], bk)
        queries = [first_queries[:]] + [
            other_queries[:, b * P : (b + 1) * P] for b in range(M_BLOCKS - 1)
        ]

        kk_bank = psum.tile([P, N], F32, name="kk_bank")
        for half, half_keys in zip(halves, raw_keys):
            nc.tensor.matmul(kk_bank[:, half], weights[:], half_keys[:], start=True, stop=True)
        kk = held.tile([P, N], BF16, name="kk")
        nc.vector.tensor_scalar_add(kk[:], kk_bank[:], bias[:, 0:1])

        def store_scaled(b, columns, bank, scores):
            rows = out[b * P : (b + 1) * P, columns]
            if b % 2 == 0:
                nc.vector.tensor_scalar_mul(scores, bank, 1.0 / math.sqrt(D))
                nc.sync.dma_start(rows, scores)
            else:
                nc.scalar.mul(scores, bank, 1.0 / math.sqrt(D))
                nc.scalar.dma_start(rows, scores)

        banks = [psum.tile([P, N], F32, name=f"bank{b}") for b in range(EARLY)]
        for b in range(EARLY):
            nc.tensor.matmul(
                banks[b][:], queries[b], table[:].indirect(offsets[:]), start=True, stop=False
            )

        for b in range(EARLY):
            for first in range(0, N, PIECE):
                columns = slice(first, min(first + PIECE, N))
                nc.tensor.matmul(
                    banks[b][:, columns],
                    queries[b],
                    kk[:, columns],
                    start=False,
                    stop=(first + PIECE >= N),
                )
            scores = staging.tile([P, N], F32, name="scores")
            for columns in halves:
                store_scaled(b, columns, banks[b][:, columns], scores[:, columns])

        late = [(b, i) for i in range(2) for b in range(EARLY, M_BLOCKS)]
        half_banks = {
            (b, i): psum.tile([P, N // 2], F32, name=f"half_bank{b}_{i}")
            for b, i in late
        }
        for b, i in late:
            nc.tensor.matmul(
                half_banks[b, i][:],
                queries[b],
                kk[:, halves[i]],
                start=True,
                stop=False,
            )
        for b, i in late:
            nc.tensor.matmul(
                half_banks[b, i][:],
                queries[b],
                table[:].indirect(offsets[:, halves[i].start // 16 : halves[i].stop // 16]),
                start=False,
                stop=True,
            )
            half_scores = held.tile([P, N // 2], F32, name=f"half_scores{b}_{i}")
            store_scaled(b, halves[i], half_banks[b, i][:], half_scores[:])
